import numpy as np
import ml_dtypes


def mxq(x, axis, fmt="e4m3"):
    dtype, down = {"e4m3": (ml_dtypes.float8_e4m3fn, 7), "e5m2": (ml_dtypes.float8_e5m2, 14)}[fmt]
    v = np.moveaxis(np.asarray(x, np.float32).astype(ml_dtypes.bfloat16).astype(np.float64), axis, -1)
    blocks = v.reshape(v.shape[:-1] + (-1, 32))
    amax = np.abs(blocks).max(-1, keepdims=True)
    byte = np.maximum(np.where(amax > 0, np.frexp(amax)[1] - 1 + 127, 0) - down, 1)
    scale = np.exp2(byte - 127.0)
    codes = (blocks / scale).astype(np.float32).astype(dtype).astype(np.float64)
    return np.moveaxis((codes * scale).reshape(v.shape), -1, axis)


WIDE = False


def mx_kscale(k):
    if not WIDE:
        return np.ones(k)
    levels = np.array([10, -10, 5, -5, 0])
    a = np.random.permutation(np.resize(levels, k // 512 * 4)).reshape(k // 512, 4)
    idx = np.arange(k)
    return np.exp2(a[idx // 512, idx % 128 // 32])


BF16 = ml_dtypes.bfloat16


def bf(x):
    return np.asarray(x, np.float32).astype(BF16)


def f64(x):
    return np.asarray(x).astype(np.float64)


E2M1 = np.array([0.0, 0.5, 1.0, 1.5, 2.0, 3.0, 4.0, 6.0, -0.0, -0.5, -1.0, -1.5, -2.0, -3.0, -4.0, -6.0])


def pack_weight(w, fmt):
    k, n = w.shape
    w = f64(bf(w)).reshape(k // 32, 32, n)
    amax = np.abs(w).max(1)
    if fmt == "e4m3":
        byte = np.frexp(amax)[1] - 1 + 127 - 7
    else:
        mant, ex = np.frexp(amax / 6.0)
        byte = np.where(mant > 0.5, ex, ex - 1) + 127
    byte = np.clip(np.where(amax > 0, byte, 1), 1, 254)
    scaled = (w * np.exp2(127.0 - byte)[:, None, :]).reshape(k, n).astype(np.float32)
    by_word = np.ascontiguousarray(scaled.reshape(k // 512, 128, 4, n).transpose(0, 1, 3, 2))
    if fmt == "e4m3":
        words = by_word.astype(ml_dtypes.float8_e4m3fn).view(np.uint8)
    else:
        c = by_word.astype(ml_dtypes.float4_e2m1fn).view(np.uint8) & 0xF
        words = c[..., 0::2] | (c[..., 1::2] << 4)
    return np.ascontiguousarray(words), np.ascontiguousarray(byte.astype(np.uint8).reshape(k // 512, 16, n))


def unpack_weight(words, scales, fmt):
    g, p, n, _ = words.shape
    if fmt == "e4m3":
        vals = np.ascontiguousarray(words).view(ml_dtypes.float8_e4m3fn).astype(np.float64)
    else:
        nib = np.empty((g, p, n, 4), np.uint8)
        nib[..., 0::2] = words & 0xF
        nib[..., 1::2] = words >> 4
        vals = E2M1[nib]
    vals = vals * np.repeat(np.exp2(scales.astype(np.float64) - 127.0), 8, axis=1)[..., None]
    return vals.transpose(0, 1, 3, 2).reshape(g * 512, n)

def pack4(w):
    words, scales = pack_weight(w, "e2m1")
    return words.reshape(words.shape[0], 128, -1), scales


def unpack4(words, scales):
    return unpack_weight(words.reshape(words.shape[0], 128, -1, 2), scales, "e2m1")


B, C, T, H = 4, 256, 2048, 1024
EPS_LN = 1e-5
EPS_STD = 1e-5


def ln_dim1(z, g, b):
    mu = z.mean(axis=1, keepdims=True)
    var = ((z - mu) ** 2).mean(axis=1, keepdims=True)
    return (z - mu) / np.sqrt(var + EPS_LN) * g[None, :, None] + b[None, :, None]


def stats(x, m):
    mean = (m * x).sum(axis=2)
    std = np.sqrt(np.maximum((m * x * x).sum(axis=2) - mean ** 2, EPS_STD))
    return mean, std


def setup_inputs():
    s = mx_kscale(H)
    drop = np.random.randint(B, size=T)
    mask = (np.arange(B)[:, None, None] != drop[None, None, :]) * 1.0
    off = 0.5 * np.random.standard_normal((B, C, 1))
    gain = 0.5 + np.random.random((B, C, 1))
    pad = np.random.standard_normal((B, C, 1)) * (1.0 - mask)
    x = off + gain * np.random.standard_normal((B, C, T)) + pad
    h = bf(np.tanh(np.random.standard_normal((B, H, T))) * s[None, :, None])
    w2 = np.random.standard_normal((C, H)) * 3.0 / np.sqrt(H) / s[None, :]
    w2_words, w2_scales = pack4(np.ascontiguousarray(w2.T))
    return {"h": h,
            "x": bf(x),
            "mask": bf(mask),
            "w2_words": w2_words,
            "w2_scales": w2_scales,
            "b2": bf(0.1 * np.random.standard_normal(C)),
            "g2": bf(1.0 + 0.1 * np.random.standard_normal(2 * C)),
            "be2": bf(0.1 * np.random.standard_normal(2 * C))}


def reference(h, x, mask, w2_words, w2_scales, b2, g2, be2):
    x, mask = f64(x), f64(mask)
    alpha = (unpack4(w2_words, w2_scales).T @ mxq(f64(h), 1, "e4m3")) + f64(b2)[None, :, None]
    alpha = np.where(mask == 0, -np.inf, alpha)
    e = np.exp(alpha - alpha.max(axis=2, keepdims=True))
    alpha = e / e.sum(axis=2, keepdims=True)
    mean, std = stats(x, alpha)
    out = np.concatenate([mean, std], axis=1)[:, :, None]
    return ln_dim1(out, f64(g2), f64(be2))

@@ -1,0 +1,283 @@
+import concourse.bass as bass
+import concourse.mybir as mybir
+import concourse.tile as tile
+from concourse.masks import make_identity
+
+FLOPS = 2 * 4 * 256 * 1024 * 2048
+
+F32 = mybir.dt.float32
+BF16 = mybir.dt.bfloat16
+I32 = mybir.dt.int32
+U32 = mybir.dt.uint32
+U8 = mybir.dt.uint8
+FP8X4 = mybir.dt.float8_e4m3fn_x4
+FP4X4 = mybir.dt.float4_e2m1fn_x4
+ALU = mybir.AluOpType
+ACT = mybir.ActivationFunctionType
+AX = mybir.AxisListType
+
+P = 128
+PACK = 4
+K_PASS = P * PACK
+B, C, T, H = 4, 256, 2048, 1024
+PASSES = H // K_PASS
+HALVES = C // P
+FRAMES = 512
+CHUNKS = T // FRAMES
+EPS_LN = 1e-5
+EPS_STD = 1e-5
+MASKED = 1.0e30
+
+
+SLOTS = B * CHUNKS
+LOAD_AHEAD = 3
+
+
+def tile_attentivestatspool_pb_t_kernel(
+    tc, h, x, mask, w2_words, w2_scales, b2, g2, be2, out
+):
+    nc = tc.nc
+    with tc.tile_pool(name="const", bufs=1) as const, tc.tile_pool(
+        name="raw", bufs=8
+    ) as raw_pool, tc.tile_pool(name="grouped", bufs=4) as grouped_pool, tc.tile_pool(
+        name="quant", bufs=3
+    ) as quant, tc.tile_pool(name="maskrows", bufs=2) as mask_pool, tc.tile_pool(
+        name="feat", bufs=3
+    ) as feat, tc.tile_pool(name="score", bufs=4) as score, tc.tile_pool(
+        name="prod", bufs=2
+    ) as prod, tc.psum_pool(name="acc", bufs=6) as acc_pool, tc.psum_pool(
+        name="tail", bufs=1
+    ) as tail_psum, tc.manual_schedule():
+        w_words = const.tile([P, PASSES, 2 * C], U8, align_bytes=64)
+        nc.sync.dma_start(
+            out=w_words[:].bitcast(I32),
+            in_=w2_words.bitcast(I32).rearrange("g p n -> p g n"),
+        )
+        w_planes = const.tile([P, PASSES, C], U8, align_bytes=64)
+        nc.vector.memset(w_planes[:].rearrange("p g n -> p (g n)").bitcast(I32), 0)
+        for q in range(4):
+            nc.sync.dma_start(
+                out=w_planes[32 * q : 32 * q + 4].bitcast(I32),
+                in_=w2_scales.bitcast(I32)[:, 4 * q : 4 * q + 4, :].rearrange(
+                    "g r n -> r g n"
+                ),
+            )
+
+        averager = const.tile([P, P], F32)
+        nc.vector.memset(averager[:], 1.0 / (2 * C))
+        ident = const.tile([P, P], F32)
+        make_identity(nc, ident[:])
+        padded = const.tile([P, P], F32)
+        nc.vector.memset(padded[:], 0.0)
+        sum_e = const.tile([P, B, HALVES], F32)
+        sum_ex = const.tile([P, B, HALVES], F32)
+        sum_exx = const.tile([P, B, HALVES], F32)
+
+        raw = {}
+        grouped = {}
+        codes = {}
+        planes = {}
+        acc = {}
+        penalty = {}
+        x_sb = {}
+        scores = {}
+        neg_max = {}
+        ex = {}
+
+        def load(s):
+            b, c = divmod(s, CHUNKS)
+            h_rows = h[b].rearrange("(g p j) n -> g p j n", p=P, j=PACK)
+            for g in range(PASSES):
+                raw[s, g] = raw_pool.tile([P, PACK, FRAMES], BF16, name="raw")
+                nc.sync.dma_start(
+                    out=raw[s, g][:], in_=h_rows[g, :, :, c * FRAMES : (c + 1) * FRAMES]
+                )
+            if c == 0:
+                mask_rows = mask_pool.tile([P, T], BF16, name="mask_rows")
+                nc.sync.dma_start(out=mask_rows[:], in_=mask[b, 0, :].partition_broadcast(P))
+                penalty[b] = mask_pool.tile([P, T], BF16, name="penalty")
+                nc.gpsimd.tensor_scalar(
+                    out=penalty[b][:],
+                    in0=mask_rows[:],
+                    scalar1=MASKED,
+                    scalar2=-MASKED,
+                    op0=ALU.mult,
+                    op1=ALU.add,
+                )
+            if c == CHUNKS - 1:
+                x_sb[b] = feat.tile([P, HALVES, T], BF16, name="x_sb")
+                nc.sync.dma_start(
+                    out=x_sb[b][:], in_=x[b].rearrange("(hf p) n -> p hf n", p=P)
+                )
+
+        def regroup(s):
+            grouped[s] = grouped_pool.tile(
+                [P, PASSES, FRAMES, PACK], BF16, name="grouped", align_bytes=64
+            )
+            for g in range(PASSES):
+                dst = grouped[s][:, g].rearrange("p (c i) j -> p c j i", i=4)
+                src = raw[s, g][:].rearrange("p j (c i) -> p c j i", i=4)
+                if s < CHUNKS and g == 1:
+                    nc.vector.tensor_copy(out=dst, in_=src)
+                else:
+                    nc.scalar.copy(out=dst, in_=src)
+
+        def quantise(s):
+            codes[s] = quant.tile([P, PASSES * FRAMES], U32, name="codes", align_bytes=64)
+            planes[s] = quant.tile([P, PASSES * FRAMES], U8, name="planes", align_bytes=64)
+            nc.vector.quantize_mx(
+                out=codes[s][:].bitcast(FP8X4),
+                scales=planes[s][:],
+                in_=grouped[s][:].rearrange("p g n j -> p (g n j)"),
+            )
+
+        def multiply(s):
+            for hf in range(HALVES):
+                acc[s, hf] = acc_pool.tile([P, FRAMES], F32, name="acc")
+                for g in range(PASSES):
+                    nc.tensor.matmul_mx(
+                        out=acc[s, hf][:],
+                        lhsT=w_words[:, g, 2 * P * hf : 2 * P * (hf + 1)].bitcast(FP4X4),
+                        lhsT_scale=w_planes[:, g, P * hf : P * (hf + 1)],
+                        rhs=codes[s][:, g * FRAMES : (g + 1) * FRAMES].bitcast(FP8X4),
+                        rhs_scale=planes[s][:, g * FRAMES : (g + 1) * FRAMES],
+                        start=(g == 0),
+                        stop=(g == PASSES - 1),
+                    )
+
+        def mask_scores(s):
+            b, c = divmod(s, CHUNKS)
+            frames = slice(c * FRAMES, (c + 1) * FRAMES)
+            for hf in range(HALVES):
+                if c == 0:
+                    scores[b, hf] = score.tile([P, T], F32, name="scores")
+                nc.vector.tensor_tensor(
+                    out=scores[b, hf][:, frames],
+                    in0=acc[s, hf][:],
+                    in1=penalty[b][:, frames],
+                    op=ALU.add,
+                )
+
+        def pool_step(b, step):
+            for hf in range(HALVES):
+                if step == 0:
+                    neg_max[b, hf] = prod.tile([P, 1], F32, name="neg_max")
+                    nc.vector.tensor_reduce(
+                        out=neg_max[b, hf][:],
+                        in_=scores[b, hf][:],
+                        axis=AX.X,
+                        op=ALU.max,
+                        negate=True,
+                    )
+                if step == 1:
+                    nc.scalar.activation(
+                        out=scores[b, hf][:],
+                        in_=scores[b, hf][:],
+                        func=ACT.Exp,
+                        bias=neg_max[b, hf][:],
+                        scale=1.0,
+                        accum_out=sum_e[:, b, hf : hf + 1],
+                    )
+                if step == 2:
+                    ex[b, hf] = prod.tile([P, T], F32, name="ex")
+                    nc.vector.scalar_tensor_tensor(
+                        out=ex[b, hf][:],
+                        in0=scores[b, hf][:],
+                        scalar=1.0,
+                        in1=x_sb[b][:, hf, :],
+                        op0=ALU.mult,
+                        op1=ALU.mult,
+                        accum_out=sum_ex[:, b, hf : hf + 1],
+                    )
+                if step == 3:
+                    exx = prod.tile([P, T], F32, name="exx")
+                    nc.vector.scalar_tensor_tensor(
+                        out=exx[:],
+                        in0=ex[b, hf][:],
+                        scalar=1.0,
+                        in1=x_sb[b][:, hf, :],
+                        op0=ALU.mult,
+                        op1=ALU.mult,
+                        accum_out=sum_exx[:, b, hf : hf + 1],
+                    )
+
+        for s in range(LOAD_AHEAD):
+            load(s)
+        regroup(0)
+        for s in range(SLOTS):
+            b, c = divmod(s, CHUNKS)
+            if s + LOAD_AHEAD < SLOTS:
+                load(s + LOAD_AHEAD)
+            if s + 1 < SLOTS:
+                regroup(s + 1)
+            quantise(s)
+            multiply(s)
+            if s > 0:
+                mask_scores(s - 1)
+            if b > 0:
+                pool_step(b - 1, c)
+        mask_scores(SLOTS - 1)
+        for step in range(CHUNKS):
+            pool_step(B - 1, step)
+
+        gain = const.tile([4 * B, P], BF16)
+        offset = const.tile([4 * B, P], BF16)
+        for b in range(B):
+            nc.sync.dma_start(
+                out=gain[4 * b : 4 * b + 4, :], in_=g2.rearrange("(q p) -> q p", p=P)
+            )
+            nc.sync.dma_start(
+                out=offset[4 * b : 4 * b + 4, :], in_=be2.rearrange("(q p) -> q p", p=P)
+            )
+
+        v = const.tile([P, B, 4], F32)
+        inv_e = const.tile([P, B, HALVES], F32)
+        nc.vector.reciprocal(out=inv_e[:], in_=sum_e[:])
+        nc.vector.tensor_mul(out=v[:, :, 0:HALVES], in0=sum_ex[:], in1=inv_e[:])
+        second = const.tile([P, B, HALVES], F32)
+        nc.vector.tensor_mul(out=second[:], in0=sum_exx[:], in1=inv_e[:])
+        mean_sq = const.tile([P, B, HALVES], F32)
+        nc.vector.tensor_mul(out=mean_sq[:], in0=v[:, :, 0:HALVES], in1=v[:, :, 0:HALVES])
+        nc.vector.tensor_sub(out=second[:], in0=second[:], in1=mean_sq[:])
+        nc.vector.tensor_scalar_max(out=second[:], in0=second[:], scalar1=EPS_STD)
+        std = const.tile([P, B, HALVES], F32)
+        nc.scalar.sqrt(out=std[:], in_=second[:])
+        nc.vector.tensor_copy(out=v[:, :, HALVES : 2 * HALVES], in_=std[:])
+
+        row_sum = const.tile([P, B], F32)
+        nc.vector.tensor_reduce(out=row_sum[:], in_=v[:], axis=AX.X, op=ALU.add)
+        mu = tail_psum.tile([P, B], F32, tag="moment")
+        nc.tensor.matmul(out=mu[:], lhsT=averager[:], rhs=row_sum[:], start=True, stop=True)
+        centred = const.tile([P, B, 4], F32)
+        nc.vector.tensor_tensor(
+            out=centred[:],
+            in0=v[:],
+            in1=mu[:].unsqueeze(2).to_broadcast([P, B, 4]),
+            op=ALU.subtract,
+        )
+        squares = const.tile([P, B, 4], F32)
+        nc.vector.tensor_mul(out=squares[:], in0=centred[:], in1=centred[:])
+        row_sq = const.tile([P, B], F32)
+        nc.vector.tensor_reduce(out=row_sq[:], in_=squares[:], axis=AX.X, op=ALU.add)
+        var = tail_psum.tile([P, B], F32, tag="moment")
+        nc.tensor.matmul(out=var[:], lhsT=averager[:], rhs=row_sq[:], start=True, stop=True)
+        spread = const.tile([P, B], F32)
+        nc.vector.tensor_scalar_add(out=spread[:], in0=var[:], scalar1=EPS_LN)
+        nc.scalar.sqrt(out=spread[:], in_=spread[:])
+        inv_spread = const.tile([P, B], F32)
+        nc.vector.reciprocal(out=inv_spread[:], in_=spread[:])
+        nc.vector.tensor_tensor(
+            out=padded[:, 0 : 4 * B].rearrange("p (b q) -> p b q", q=4),
+            in0=centred[:],
+            in1=inv_spread[:].unsqueeze(2).to_broadcast([P, B, 4]),
+            op=ALU.mult,
+        )
+
+        turned = tail_psum.tile([P, P], F32)
+        nc.tensor.transpose(out=turned[:], in_=padded[:], identity=ident[:])
+        result = const.tile([4 * B, P], F32)
+        nc.vector.tensor_tensor(
+            out=result[:], in0=turned[0 : 4 * B, :], in1=gain[:], op=ALU.mult
+        )
+        nc.vector.tensor_tensor(out=result[:], in0=result[:], in1=offset[:], op=ALU.add)
+        nc.sync.dma_start(out=out.rearrange("b (q p) o -> (b q) (p o)", p=P), in_=result[:])

@@ -48,36 +48,20 @@ def tile_attentivestatspool_pb_t_kernel(
     ) as prod, tc.psum_pool(name="acc", bufs=6) as acc_pool, tc.psum_pool(
         name="tail", bufs=1
     ) as tail_psum, tc.manual_schedule():
-        w_words = const.tile([P, PASSES, 2 * C], U8, align_bytes=64)
-        nc.sync.dma_start(
-            out=w_words[:].bitcast(I32),
-            in_=w2_words.bitcast(I32).rearrange("g p n -> p g n"),
-        )
-        w_planes = const.tile([P, PASSES, C], U8, align_bytes=64)
-        nc.vector.memset(w_planes[:].rearrange("p g n -> p (g n)").bitcast(I32), 0)
-        for q in range(4):
-            nc.sync.dma_start(
-                out=w_planes[32 * q : 32 * q + 4].bitcast(I32),
-                in_=w2_scales.bitcast(I32)[:, 4 * q : 4 * q + 4, :].rearrange(
-                    "g r n -> r g n"
-                ),
-            )
-
-        averager = const.tile([P, P], F32)
-        nc.vector.memset(averager[:], 1.0 / (2 * C))
         ident = const.tile([P, P], F32)
         make_identity(nc, ident[:])
-        padded = const.tile([P, P], F32)
-        nc.vector.memset(padded[:], 0.0)
-        sum_e = const.tile([P, B, HALVES], F32)
-        sum_ex = const.tile([P, B, HALVES], F32)
-        sum_exx = const.tile([P, B, HALVES], F32)
+        v = const.tile([P, 2 * HALVES, P], F32)
+        nc.gpsimd.memset(v[:], 0.0)
+        sum_e = const.tile([P, HALVES, B], F32)
+        sum_ex = const.tile([P, HALVES, B], F32)
+        sum_exx = const.tile([P, HALVES, B], F32)
 
         raw = {}
         grouped = {}
         codes = {}
         planes = {}
         acc = {}
+        mask_rows = {}
         penalty = {}
         x_sb = {}
         scores = {}
@@ -92,17 +76,10 @@ def tile_attentivestatspool_pb_t_kernel(
                 nc.sync.dma_start(
                     out=raw[s, g][:], in_=h_rows[g, :, :, c * FRAMES : (c + 1) * FRAMES]
                 )
-            if c == 0:
-                mask_rows = mask_pool.tile([P, T], BF16, name="mask_rows")
-                nc.sync.dma_start(out=mask_rows[:], in_=mask[b, 0, :].partition_broadcast(P))
-                penalty[b] = mask_pool.tile([P, T], BF16, name="penalty")
-                nc.gpsimd.tensor_scalar(
-                    out=penalty[b][:],
-                    in0=mask_rows[:],
-                    scalar1=MASKED,
-                    scalar2=-MASKED,
-                    op0=ALU.mult,
-                    op1=ALU.add,
+            if c == 1:
+                mask_rows[b] = mask_pool.tile([P, T], BF16, name="mask_rows")
+                nc.sync.dma_start(
+                    out=mask_rows[b][:], in_=mask[b, 0, :].partition_broadcast(P)
                 )
             if c == CHUNKS - 1:
                 x_sb[b] = feat.tile([P, HALVES, T], BF16, name="x_sb")
@@ -121,6 +98,17 @@ def tile_attentivestatspool_pb_t_kernel(
                     nc.vector.tensor_copy(out=dst, in_=src)
                 else:
                     nc.scalar.copy(out=dst, in_=src)
+
+        def make_penalty(b):
+            penalty[b] = mask_pool.tile([P, T], BF16, name="penalty")
+            nc.vector.tensor_scalar(
+                out=penalty[b][:],
+                in0=mask_rows[b][:],
+                scalar1=MASKED,
+                scalar2=-MASKED,
+                op0=ALU.mult,
+                op1=ALU.add,
+            )
 
         def quantise(s):
             codes[s] = quant.tile([P, PASSES * FRAMES], U32, name="codes", align_bytes=64)
@@ -176,7 +164,7 @@ def tile_attentivestatspool_pb_t_kernel(
                         func=ACT.Exp,
                         bias=neg_max[b, hf][:],
                         scale=1.0,
-                        accum_out=sum_e[:, b, hf : hf + 1],
+                        accum_out=sum_e[:, hf, b : b + 1],
                     )
                 if step == 2:
                     ex[b, hf] = prod.tile([P, T], F32, name="ex")
@@ -187,7 +175,7 @@ def tile_attentivestatspool_pb_t_kernel(
                         in1=x_sb[b][:, hf, :],
                         op0=ALU.mult,
                         op1=ALU.mult,
-                        accum_out=sum_ex[:, b, hf : hf + 1],
+                        accum_out=sum_ex[:, hf, b : b + 1],
                     )
                 if step == 3:
                     exx = prod.tile([P, T], F32, name="exx")
@@ -198,86 +186,97 @@ def tile_attentivestatspool_pb_t_kernel(
                         in1=x_sb[b][:, hf, :],
                         op0=ALU.mult,
                         op1=ALU.mult,
-                        accum_out=sum_exx[:, b, hf : hf + 1],
+                        accum_out=sum_exx[:, hf, b : b + 1],
                     )
 
-        for s in range(LOAD_AHEAD):
+        load(0)
+        load(1)
+        w_words = const.tile([P, PASSES, 2 * C], U8, align_bytes=64)
+        nc.sync.dma_start(
+            out=w_words[:].bitcast(I32),
+            in_=w2_words.bitcast(I32).rearrange("g p n -> p g n"),
+        )
+        w_planes = const.tile([P, PASSES, C], U8, align_bytes=64)
+        nc.vector.memset(w_planes[:].rearrange("p g n -> p (g n)").bitcast(I32), 0)
+        for q in range(4):
+            nc.sync.dma_start(
+                out=w_planes[32 * q : 32 * q + 4].bitcast(I32),
+                in_=w2_scales.bitcast(I32)[:, 4 * q : 4 * q + 4, :].rearrange(
+                    "g r n -> r g n"
+                ),
+            )
+
+        for s in range(2, LOAD_AHEAD):
             load(s)
         regroup(0)
         for s in range(SLOTS):
             b, c = divmod(s, CHUNKS)
             if s + LOAD_AHEAD < SLOTS:
                 load(s + LOAD_AHEAD)
-            if s + 1 < SLOTS:
-                regroup(s + 1)
             quantise(s)
             multiply(s)
+            if s + 1 < SLOTS:
+                regroup(s + 1)
+            if c == 0:
+                make_penalty(b)
             if s > 0:
                 mask_scores(s - 1)
             if b > 0:
                 pool_step(b - 1, c)
+        gain = const.tile([B, 2 * C], BF16)
+        nc.sync.dma_start(out=gain[:], in_=g2.partition_broadcast(B))
+        offset = const.tile([B, 2 * C], BF16)
+        nc.sync.dma_start(out=offset[:], in_=be2.partition_broadcast(B))
+
         mask_scores(SLOTS - 1)
-        for step in range(CHUNKS):
-            pool_step(B - 1, step)
-
-        gain = const.tile([4 * B, P], BF16)
-        offset = const.tile([4 * B, P], BF16)
-        for b in range(B):
-            nc.sync.dma_start(
-                out=gain[4 * b : 4 * b + 4, :], in_=g2.rearrange("(q p) -> q p", p=P)
-            )
-            nc.sync.dma_start(
-                out=offset[4 * b : 4 * b + 4, :], in_=be2.rearrange("(q p) -> q p", p=P)
-            )
-
-        v = const.tile([P, B, 4], F32)
-        inv_e = const.tile([P, B, HALVES], F32)
+        pool_step(B - 1, 0)
+        pool_step(B - 1, 1)
+        warm = const.tile([P, 1], F32)
+        nc.scalar.sqrt(out=warm[:], in_=ident[:, 0:1])
+        pool_step(B - 1, 2)
+        inv_e = const.tile([P, HALVES, B], F32)
         nc.vector.reciprocal(out=inv_e[:], in_=sum_e[:])
-        nc.vector.tensor_mul(out=v[:, :, 0:HALVES], in0=sum_ex[:], in1=inv_e[:])
-        second = const.tile([P, B, HALVES], F32)
-        nc.vector.tensor_mul(out=second[:], in0=sum_exx[:], in1=inv_e[:])
-        mean_sq = const.tile([P, B, HALVES], F32)
-        nc.vector.tensor_mul(out=mean_sq[:], in0=v[:, :, 0:HALVES], in1=v[:, :, 0:HALVES])
-        nc.vector.tensor_sub(out=second[:], in0=second[:], in1=mean_sq[:])
-        nc.vector.tensor_scalar_max(out=second[:], in0=second[:], scalar1=EPS_STD)
-        std = const.tile([P, B, HALVES], F32)
-        nc.scalar.sqrt(out=std[:], in_=second[:])
-        nc.vector.tensor_copy(out=v[:, :, HALVES : 2 * HALVES], in_=std[:])
+        nc.vector.tensor_mul(out=v[:, 0:HALVES, 0:B], in0=sum_ex[:], in1=inv_e[:])
+        mean_sq = const.tile([P, HALVES, B], F32)
+        nc.vector.tensor_mul(out=mean_sq[:], in0=v[:, 0:HALVES, 0:B], in1=v[:, 0:HALVES, 0:B])
+        pool_step(B - 1, 3)
 
-        row_sum = const.tile([P, B], F32)
-        nc.vector.tensor_reduce(out=row_sum[:], in_=v[:], axis=AX.X, op=ALU.add)
-        mu = tail_psum.tile([P, B], F32, tag="moment")
-        nc.tensor.matmul(out=mu[:], lhsT=averager[:], rhs=row_sum[:], start=True, stop=True)
-        centred = const.tile([P, B, 4], F32)
-        nc.vector.tensor_tensor(
-            out=centred[:],
-            in0=v[:],
-            in1=mu[:].unsqueeze(2).to_broadcast([P, B, 4]),
-            op=ALU.subtract,
-        )
-        squares = const.tile([P, B, 4], F32)
-        nc.vector.tensor_mul(out=squares[:], in0=centred[:], in1=centred[:])
-        row_sq = const.tile([P, B], F32)
-        nc.vector.tensor_reduce(out=row_sq[:], in_=squares[:], axis=AX.X, op=ALU.add)
-        var = tail_psum.tile([P, B], F32, tag="moment")
-        nc.tensor.matmul(out=var[:], lhsT=averager[:], rhs=row_sq[:], start=True, stop=True)
-        spread = const.tile([P, B], F32)
-        nc.vector.tensor_scalar_add(out=spread[:], in0=var[:], scalar1=EPS_LN)
-        nc.scalar.sqrt(out=spread[:], in_=spread[:])
-        inv_spread = const.tile([P, B], F32)
-        nc.vector.reciprocal(out=inv_spread[:], in_=spread[:])
-        nc.vector.tensor_tensor(
-            out=padded[:, 0 : 4 * B].rearrange("p (b q) -> p b q", q=4),
-            in0=centred[:],
-            in1=inv_spread[:].unsqueeze(2).to_broadcast([P, B, 4]),
-            op=ALU.mult,
-        )
+        spread = const.tile([P, HALVES, B], F32)
+        nc.vector.tensor_mul(out=spread[:], in0=sum_exx[:], in1=inv_e[:])
+        nc.vector.tensor_sub(out=spread[:], in0=spread[:], in1=mean_sq[:])
+        nc.vector.tensor_scalar_max(out=spread[:], in0=spread[:], scalar1=EPS_STD)
+        nc.scalar.sqrt(out=v[:, HALVES : 2 * HALVES, 0:B], in_=spread[:])
 
-        turned = tail_psum.tile([P, P], F32)
-        nc.tensor.transpose(out=turned[:], in_=padded[:], identity=ident[:])
-        result = const.tile([4 * B, P], F32)
-        nc.vector.tensor_tensor(
-            out=result[:], in0=turned[0 : 4 * B, :], in1=gain[:], op=ALU.mult
+        turned = tail_psum.tile([P, 2 * C], F32)
+        for q in range(2 * HALVES):
+            nc.tensor.transpose(
+                out=turned[:, q * P : (q + 1) * P], in_=v[:, q, :], identity=ident[:]
+            )
+
+        stats = const.tile([B, 6], F32)
+        nc.vector.bn_stats(out=stats[:], in_=turned[0:B, :])
+        mean_var = const.tile([B, 2], F32)
+        nc.vector.bn_aggr(out=mean_var[:], in_=stats[:])
+        sd = const.tile([B, 1], F32)
+        nc.vector.tensor_scalar_add(out=sd[:], in0=mean_var[:, 1:2], scalar1=EPS_LN)
+        nc.scalar.sqrt(out=sd[:], in_=sd[:])
+        inv_sd = const.tile([B, 1], F32)
+        nc.vector.reciprocal(out=inv_sd[:], in_=sd[:])
+        result = const.tile([B, 2 * C], F32)
+        nc.vector.scalar_tensor_tensor(
+            out=result[:],
+            in0=turned[0:B, :],
+            scalar=mean_var[:, 0:1],
+            in1=gain[:],
+            op0=ALU.subtract,
+            op1=ALU.mult,
         )
-        nc.vector.tensor_tensor(out=result[:], in0=result[:], in1=offset[:], op=ALU.add)
-        nc.sync.dma_start(out=out.rearrange("b (q p) o -> (b q) (p o)", p=P), in_=result[:])
+        nc.vector.scalar_tensor_tensor(
+            out=result[:],
+            in0=result[:],
+            scalar=inv_sd[:],
+            in1=offset[:],
+            op0=ALU.mult,
+            op1=ALU.add,
+        )
+        nc.sync.dma_start(out=out.rearrange("b n o -> b (n o)"), in_=result[:])

@@ -31,6 +31,7 @@ MASKED = 1.0e30
 
 SLOTS = B * CHUNKS
 LOAD_AHEAD = 3
+HELPED_SLOTS = 5
 
 
 def tile_attentivestatspool_pb_t_kernel(
@@ -78,14 +79,17 @@ def tile_attentivestatspool_pb_t_kernel(
                 )
             if c == 1:
                 mask_rows[b] = mask_pool.tile([P, T], BF16, name="mask_rows")
-                nc.sync.dma_start(
+                nc.gpsimd.dma_start(
                     out=mask_rows[b][:], in_=mask[b, 0, :].partition_broadcast(P)
                 )
-            if c == CHUNKS - 1:
-                x_sb[b] = feat.tile([P, HALVES, T], BF16, name="x_sb")
-                nc.sync.dma_start(
-                    out=x_sb[b][:], in_=x[b].rearrange("(hf p) n -> p hf n", p=P)
-                )
+            if c == 1 and b > 0:
+                load_x(b - 1)
+            if s == SLOTS - 1:
+                load_x(b)
+
+        def load_x(b):
+            x_sb[b] = feat.tile([P, HALVES, T], BF16, name="x_sb")
+            nc.sync.dma_start(out=x_sb[b][:], in_=x[b].rearrange("(hf p) n -> p hf n", p=P))
 
         def regroup(s):
             grouped[s] = grouped_pool.tile(
@@ -94,7 +98,7 @@ def tile_attentivestatspool_pb_t_kernel(
             for g in range(PASSES):
                 dst = grouped[s][:, g].rearrange("p (c i) j -> p c j i", i=4)
                 src = raw[s, g][:].rearrange("p j (c i) -> p c j i", i=4)
-                if s < CHUNKS and g == 1:
+                if s < HELPED_SLOTS and g == 1:
                     nc.vector.tensor_copy(out=dst, in_=src)
                 else:
                     nc.scalar.copy(out=dst, in_=src)

@@ -105,7 +105,7 @@ def tile_attentivestatspool_pb_t_kernel(
 
         def make_penalty(b):
             penalty[b] = mask_pool.tile([P, T], BF16, name="penalty")
-            nc.vector.tensor_scalar(
+            nc.gpsimd.tensor_scalar(
                 out=penalty[b][:],
                 in0=mask_rows[b][:],
                 scalar1=MASKED,

@@ -32,6 +32,7 @@ MASKED = 1.0e30
 SLOTS = B * CHUNKS
 LOAD_AHEAD = 3
 HELPED_SLOTS = 5
+GPSIMD_CHUNK = 2
 
 
 def tile_attentivestatspool_pb_t_kernel(
@@ -40,7 +41,7 @@ def tile_attentivestatspool_pb_t_kernel(
     nc = tc.nc
     with tc.tile_pool(name="const", bufs=1) as const, tc.tile_pool(
         name="raw", bufs=8
-    ) as raw_pool, tc.tile_pool(name="grouped", bufs=4) as grouped_pool, tc.tile_pool(
+    ) as raw_pool, tc.tile_pool(name="grouped", bufs=2) as grouped_pool, tc.tile_pool(
         name="quant", bufs=3
     ) as quant, tc.tile_pool(name="maskrows", bufs=2) as mask_pool, tc.tile_pool(
         name="feat", bufs=3
@@ -79,7 +80,7 @@ def tile_attentivestatspool_pb_t_kernel(
                 )
             if c == 1:
                 mask_rows[b] = mask_pool.tile([P, T], BF16, name="mask_rows")
-                nc.gpsimd.dma_start(
+                nc.sync.dma_start(
                     out=mask_rows[b][:], in_=mask[b, 0, :].partition_broadcast(P)
                 )
             if c == 1 and b > 0:
@@ -103,15 +104,31 @@ def tile_attentivestatspool_pb_t_kernel(
                 else:
                     nc.scalar.copy(out=dst, in_=src)
 
+        def on_gpsimd(s):
+            return s >= CHUNKS and s % CHUNKS == GPSIMD_CHUNK
+
+        def regroup_on_gpsimd(s):
+            grouped[s] = grouped_pool.tile(
+                [P, PASSES, FRAMES, PACK], BF16, name="grouped", align_bytes=64
+            )
+            for g in range(PASSES):
+                nc.gpsimd.tensor_scalar(
+                    out=grouped[s][:, g],
+                    in0=raw[s, g][:].rearrange("p j n -> p n j"),
+                    scalar1=1.0,
+                    scalar2=0.0,
+                    op0=ALU.mult,
+                    op1=ALU.add,
+                )
+
         def make_penalty(b):
             penalty[b] = mask_pool.tile([P, T], BF16, name="penalty")
-            nc.gpsimd.tensor_scalar(
+            nc.scalar.activation(
                 out=penalty[b][:],
-                in0=mask_rows[b][:],
-                scalar1=MASKED,
-                scalar2=-MASKED,
-                op0=ALU.mult,
-                op1=ALU.add,
+                in_=mask_rows[b][:],
+                func=ACT.Copy,
+                scale=MASKED,
+                bias=-MASKED,
             )
 
         def quantise(s):
@@ -219,8 +236,10 @@ def tile_attentivestatspool_pb_t_kernel(
                 load(s + LOAD_AHEAD)
             quantise(s)
             multiply(s)
-            if s + 1 < SLOTS:
+            if s + 1 < SLOTS and not on_gpsimd(s + 1):
                 regroup(s + 1)
+            if s + 2 < SLOTS and on_gpsimd(s + 2):
+                regroup_on_gpsimd(s + 2)
             if c == 0:
                 make_penalty(b)
             if s > 0:

@@ -24,15 +24,20 @@ PASSES = H // K_PASS
 HALVES = C // P
 FRAMES = 512
 CHUNKS = T // FRAMES
+TILES = FRAMES // P
+UTT_TILES = T // P
 EPS_LN = 1e-5
 EPS_STD = 1e-5
 MASKED = 1.0e30
 
-
 SLOTS = B * CHUNKS
 LOAD_AHEAD = 3
-HELPED_SLOTS = 5
-GPSIMD_CHUNK = 2
+EXP_LAG = 5
+PRODUCT_LAG = 7
+STEPS = SLOTS + PRODUCT_LAG
+EARLY_SLOTS = 8
+EARLY_FRAMES = 512
+LATE_FRAMES = 336
 
 
 def tile_attentivestatspool_pb_t_kernel(
@@ -41,33 +46,37 @@ def tile_attentivestatspool_pb_t_kernel(
     nc = tc.nc
     with tc.tile_pool(name="const", bufs=1) as const, tc.tile_pool(
         name="raw", bufs=8
-    ) as raw_pool, tc.tile_pool(name="grouped", bufs=2) as grouped_pool, tc.tile_pool(
+    ) as raw_pool, tc.tile_pool(name="grouped", bufs=3) as grouped_pool, tc.tile_pool(
         name="quant", bufs=3
-    ) as quant, tc.tile_pool(name="maskrows", bufs=2) as mask_pool, tc.tile_pool(
+    ) as quant, tc.tile_pool(name="turned", bufs=2) as turned_pool, tc.tile_pool(
         name="feat", bufs=3
     ) as feat, tc.tile_pool(name="score", bufs=4) as score, tc.tile_pool(
         name="prod", bufs=2
-    ) as prod, tc.psum_pool(name="acc", bufs=6) as acc_pool, tc.psum_pool(
-        name="tail", bufs=1
-    ) as tail_psum, tc.manual_schedule():
+    ) as prod, tc.psum_pool(name="acc", bufs=4) as acc_pool, tc.psum_pool(
+        name="back", bufs=4
+    ) as back_pool, tc.manual_schedule():
         ident = const.tile([P, P], F32)
         make_identity(nc, ident[:])
+        ident_bf = const.tile([P, P], BF16)
+        make_identity(nc, ident_bf[:])
         v = const.tile([P, 2 * HALVES, P], F32)
         nc.gpsimd.memset(v[:], 0.0)
-        sum_e = const.tile([P, HALVES, B], F32)
+        sum_e4 = const.tile([P, HALVES, B, CHUNKS], F32)
         sum_ex = const.tile([P, HALVES, B], F32)
         sum_exx = const.tile([P, HALVES, B], F32)
+        neg_max4 = const.tile([P, B, HALVES, CHUNKS], F32)
+        neg_max = const.tile([P, B, HALVES], F32)
 
         raw = {}
         grouped = {}
         codes = {}
         planes = {}
         acc = {}
-        mask_rows = {}
-        penalty = {}
+        turned = {}
+        first = {}
+        again = {}
         x_sb = {}
-        scores = {}
-        neg_max = {}
+        e = {}
         ex = {}
 
         def load(s):
@@ -78,15 +87,6 @@ def tile_attentivestatspool_pb_t_kernel(
                 nc.sync.dma_start(
                     out=raw[s, g][:], in_=h_rows[g, :, :, c * FRAMES : (c + 1) * FRAMES]
                 )
-            if c == 1:
-                mask_rows[b] = mask_pool.tile([P, T], BF16, name="mask_rows")
-                nc.sync.dma_start(
-                    out=mask_rows[b][:], in_=mask[b, 0, :].partition_broadcast(P)
-                )
-            if c == 1 and b > 0:
-                load_x(b - 1)
-            if s == SLOTS - 1:
-                load_x(b)
 
         def load_x(b):
             x_sb[b] = feat.tile([P, HALVES, T], BF16, name="x_sb")
@@ -96,40 +96,16 @@ def tile_attentivestatspool_pb_t_kernel(
             grouped[s] = grouped_pool.tile(
                 [P, PASSES, FRAMES, PACK], BF16, name="grouped", align_bytes=64
             )
+            cut = (EARLY_FRAMES if s < EARLY_SLOTS else LATE_FRAMES) // 4
             for g in range(PASSES):
                 dst = grouped[s][:, g].rearrange("p (c i) j -> p c j i", i=4)
                 src = raw[s, g][:].rearrange("p j (c i) -> p c j i", i=4)
-                if s < HELPED_SLOTS and g == 1:
-                    nc.vector.tensor_copy(out=dst, in_=src)
-                else:
+                if g == 0:
                     nc.scalar.copy(out=dst, in_=src)
-
-        def on_gpsimd(s):
-            return s >= CHUNKS and s % CHUNKS == GPSIMD_CHUNK
-
-        def regroup_on_gpsimd(s):
-            grouped[s] = grouped_pool.tile(
-                [P, PASSES, FRAMES, PACK], BF16, name="grouped", align_bytes=64
-            )
-            for g in range(PASSES):
-                nc.gpsimd.tensor_scalar(
-                    out=grouped[s][:, g],
-                    in0=raw[s, g][:].rearrange("p j n -> p n j"),
-                    scalar1=1.0,
-                    scalar2=0.0,
-                    op0=ALU.mult,
-                    op1=ALU.add,
-                )
-
-        def make_penalty(b):
-            penalty[b] = mask_pool.tile([P, T], BF16, name="penalty")
-            nc.scalar.activation(
-                out=penalty[b][:],
-                in_=mask_rows[b][:],
-                func=ACT.Copy,
-                scale=MASKED,
-                bias=-MASKED,
-            )
+                else:
+                    nc.vector.tensor_copy(out=dst[:, 0:cut], in_=src[:, 0:cut])
+                    if cut < FRAMES // 4:
+                        nc.scalar.copy(out=dst[:, cut:], in_=src[:, cut:])
 
         def quantise(s):
             codes[s] = quant.tile([P, PASSES * FRAMES], U32, name="codes", align_bytes=64)
@@ -141,77 +117,119 @@ def tile_attentivestatspool_pb_t_kernel(
             )
 
         def multiply(s):
-            for hf in range(HALVES):
-                acc[s, hf] = acc_pool.tile([P, FRAMES], F32, name="acc")
-                for g in range(PASSES):
-                    nc.tensor.matmul_mx(
-                        out=acc[s, hf][:],
-                        lhsT=w_words[:, g, 2 * P * hf : 2 * P * (hf + 1)].bitcast(FP4X4),
-                        lhsT_scale=w_planes[:, g, P * hf : P * (hf + 1)],
-                        rhs=codes[s][:, g * FRAMES : (g + 1) * FRAMES].bitcast(FP8X4),
-                        rhs_scale=planes[s][:, g * FRAMES : (g + 1) * FRAMES],
-                        start=(g == 0),
-                        stop=(g == PASSES - 1),
-                    )
+            for k in range(TILES // 2):
+                acc[s, k] = acc_pool.tile([P, 2 * C], F32, name="acc")
+            for i in range(TILES):
+                for hf in range(HALVES):
+                    for g in range(PASSES):
+                        cols = slice(g * FRAMES + i * P, g * FRAMES + (i + 1) * P)
+                        at = (i % 2) * C + hf * P
+                        nc.tensor.matmul_mx(
+                            out=acc[s, i // 2][:, at : at + P],
+                            lhsT=codes[s][:, cols].bitcast(FP8X4),
+                            lhsT_scale=planes[s][:, cols],
+                            rhs=w_words[:, g, 2 * P * hf : 2 * P * (hf + 1)].bitcast(FP4X4),
+                            rhs_scale=w_planes[:, g, P * hf : P * (hf + 1)],
+                            start=(g == 0),
+                            stop=(g == PASSES - 1),
+                        )
 
-        def mask_scores(s):
+        def empty(s):
             b, c = divmod(s, CHUNKS)
-            frames = slice(c * FRAMES, (c + 1) * FRAMES)
-            for hf in range(HALVES):
-                if c == 0:
-                    scores[b, hf] = score.tile([P, T], F32, name="scores")
-                nc.vector.tensor_tensor(
-                    out=scores[b, hf][:, frames],
-                    in0=acc[s, hf][:],
-                    in1=penalty[b][:, frames],
-                    op=ALU.add,
+            if c == 0:
+                turned[b] = turned_pool.tile([P, UTT_TILES, C], F32, name="turned")
+            for i in range(TILES):
+                n = c * TILES + i
+                nc.scalar.activation(
+                    out=turned[b][:, n, :],
+                    in_=acc[s, i // 2][:, (i % 2) * C : (i % 2 + 1) * C],
+                    func=ACT.Identity,
+                    bias=penalty[:, b * UTT_TILES + n : b * UTT_TILES + n + 1],
+                    scale=1.0,
                 )
 
-        def pool_step(b, step):
+        def turn(b, c, hf):
+            bank = back_pool.tile([P, FRAMES], F32, name="back")
+            for i in range(TILES):
+                nc.tensor.transpose(
+                    out=bank[:, i * P : (i + 1) * P],
+                    in_=turned[b][:, c * TILES + i, hf * P : (hf + 1) * P],
+                    identity=ident[:],
+                )
+            return bank
+
+        def chunk_max(s):
+            b, c = divmod(s, CHUNKS)
             for hf in range(HALVES):
-                if step == 0:
-                    neg_max[b, hf] = prod.tile([P, 1], F32, name="neg_max")
-                    nc.vector.tensor_reduce(
-                        out=neg_max[b, hf][:],
-                        in_=scores[b, hf][:],
-                        axis=AX.X,
-                        op=ALU.max,
-                        negate=True,
-                    )
-                if step == 1:
-                    nc.scalar.activation(
-                        out=scores[b, hf][:],
-                        in_=scores[b, hf][:],
-                        func=ACT.Exp,
-                        bias=neg_max[b, hf][:],
-                        scale=1.0,
-                        accum_out=sum_e[:, hf, b : b + 1],
-                    )
-                if step == 2:
-                    ex[b, hf] = prod.tile([P, T], F32, name="ex")
-                    nc.vector.scalar_tensor_tensor(
-                        out=ex[b, hf][:],
-                        in0=scores[b, hf][:],
-                        scalar=1.0,
-                        in1=x_sb[b][:, hf, :],
-                        op0=ALU.mult,
-                        op1=ALU.mult,
-                        accum_out=sum_ex[:, hf, b : b + 1],
-                    )
-                if step == 3:
-                    exx = prod.tile([P, T], F32, name="exx")
-                    nc.vector.scalar_tensor_tensor(
-                        out=exx[:],
-                        in0=ex[b, hf][:],
-                        scalar=1.0,
-                        in1=x_sb[b][:, hf, :],
-                        op0=ALU.mult,
-                        op1=ALU.mult,
-                        accum_out=sum_exx[:, hf, b : b + 1],
-                    )
+                nc.vector.tensor_reduce(
+                    out=neg_max4[:, b, hf, c : c + 1],
+                    in_=first[s, hf][:],
+                    axis=AX.X,
+                    op=ALU.max,
+                    negate=True,
+                )
+            if c == CHUNKS - 1:
+                nc.vector.tensor_reduce(
+                    out=neg_max[:, b, :], in_=neg_max4[:, b], axis=AX.X, op=ALU.min
+                )
+
+        def units(step):
+            found = []
+            for b in range(B):
+                k = 2 * (step - CHUNKS * b - EXP_LAG)
+                if 0 <= k < HALVES * CHUNKS:
+                    found.extend([(b, n % CHUNKS, n // CHUNKS) for n in (k, k + 1)])
+            return found
+
+        def exponent(b, c, hf):
+            if c == 0:
+                e[b, hf] = score.tile([P, T], F32, name="e")
+            nc.scalar.activation(
+                out=e[b, hf][:, c * FRAMES : (c + 1) * FRAMES],
+                in_=again[b, c, hf][:],
+                func=ACT.Exp,
+                bias=neg_max[:, b, hf : hf + 1],
+                scale=1.0,
+                accum_out=sum_e4[:, hf, b, c : c + 1],
+            )
+
+        def product(step):
+            n = step - PRODUCT_LAG
+            if n < 0 or n >= 2 * HALVES * B:
+                return
+            b, k = divmod(n, 2 * HALVES)
+            hf, second = divmod(k, 2)
+            if not second:
+                ex[b, hf] = prod.tile([P, T], F32, name="ex")
+                nc.vector.scalar_tensor_tensor(
+                    out=ex[b, hf][:],
+                    in0=e[b, hf][:],
+                    scalar=1.0,
+                    in1=x_sb[b][:, hf, :],
+                    op0=ALU.mult,
+                    op1=ALU.mult,
+                    accum_out=sum_ex[:, hf, b : b + 1],
+                )
+            else:
+                exx = prod.tile([P, T], F32, name="exx")
+                nc.vector.scalar_tensor_tensor(
+                    out=exx[:],
+                    in0=ex[b, hf][:],
+                    scalar=1.0,
+                    in1=x_sb[b][:, hf, :],
+                    op0=ALU.mult,
+                    op1=ALU.mult,
+                    accum_out=sum_exx[:, hf, b : b + 1],
+                )
 
         load(0)
         load(1)
+        mask_rows = const.tile([P, P], BF16)
+        nc.vector.memset(mask_rows[B * UTT_TILES : P, :], 0.0)
+        nc.sync.dma_start(
+            out=mask_rows[0 : B * UTT_TILES, :],
+            in_=mask.rearrange("b o (i p) -> (b o i) p", p=P),
+        )
         w_words = const.tile([P, PASSES, 2 * C], U8, align_bytes=64)
         nc.sync.dma_start(
             out=w_words[:].bitcast(I32),
@@ -226,43 +244,63 @@ def tile_attentivestatspool_pb_t_kernel(
                     "g r n -> r g n"
                 ),
             )
-
         for s in range(2, LOAD_AHEAD):
             load(s)
+        mask_cols = back_pool.tile([P, P], BF16, name="back")
+        nc.tensor.transpose(out=mask_cols[:], in_=mask_rows[:], identity=ident_bf[:])
+        penalty = const.tile([P, B * UTT_TILES], F32)
         regroup(0)
-        for s in range(SLOTS):
-            b, c = divmod(s, CHUNKS)
-            if s + LOAD_AHEAD < SLOTS:
-                load(s + LOAD_AHEAD)
-            quantise(s)
-            multiply(s)
-            if s + 1 < SLOTS and not on_gpsimd(s + 1):
-                regroup(s + 1)
-            if s + 2 < SLOTS and on_gpsimd(s + 2):
-                regroup_on_gpsimd(s + 2)
-            if c == 0:
-                make_penalty(b)
-            if s > 0:
-                mask_scores(s - 1)
-            if b > 0:
-                pool_step(b - 1, c)
-        gain = const.tile([B, 2 * C], BF16)
-        nc.sync.dma_start(out=gain[:], in_=g2.partition_broadcast(B))
-        offset = const.tile([B, 2 * C], BF16)
-        nc.sync.dma_start(out=offset[:], in_=be2.partition_broadcast(B))
 
-        mask_scores(SLOTS - 1)
-        pool_step(B - 1, 0)
-        pool_step(B - 1, 1)
         warm = const.tile([P, 1], F32)
-        nc.scalar.sqrt(out=warm[:], in_=ident[:, 0:1])
-        pool_step(B - 1, 2)
         inv_e = const.tile([P, HALVES, B], F32)
-        nc.vector.reciprocal(out=inv_e[:], in_=sum_e[:])
-        nc.vector.tensor_mul(out=v[:, 0:HALVES, 0:B], in0=sum_ex[:], in1=inv_e[:])
         mean_sq = const.tile([P, HALVES, B], F32)
-        nc.vector.tensor_mul(out=mean_sq[:], in0=v[:, 0:HALVES, 0:B], in1=v[:, 0:HALVES, 0:B])
-        pool_step(B - 1, 3)
+        gain = const.tile([B, 2 * C], BF16)
+        offset = const.tile([B, 2 * C], BF16)
+        for step in range(STEPS):
+            if step + LOAD_AHEAD < SLOTS:
+                load(step + LOAD_AHEAD)
+            if step < SLOTS and step % CHUNKS == CHUNKS - 1:
+                load_x(step // CHUNKS)
+            if step == SLOTS - 1:
+                nc.sync.dma_start(out=gain[:], in_=g2.partition_broadcast(B))
+                nc.sync.dma_start(out=offset[:], in_=be2.partition_broadcast(B))
+            if 1 <= step <= SLOTS:
+                empty(step - 1)
+            now = units(step)
+            for b, c, hf in now:
+                again[b, c, hf] = turn(b, c, hf)
+            if step < SLOTS:
+                quantise(step)
+                multiply(step)
+            if step == 0:
+                nc.vector.tensor_scalar(
+                    out=penalty[:],
+                    in0=mask_cols[:, 0 : B * UTT_TILES],
+                    scalar1=MASKED,
+                    scalar2=-MASKED,
+                    op0=ALU.mult,
+                    op1=ALU.add,
+                )
+            if 1 <= step <= SLOTS:
+                for hf in range(HALVES):
+                    first[step - 1, hf] = turn((step - 1) // CHUNKS, (step - 1) % CHUNKS, hf)
+            for b, c, hf in now:
+                exponent(b, c, hf)
+            if step == CHUNKS * (B - 1) + EXP_LAG + CHUNKS - 1:
+                nc.scalar.sqrt(out=warm[:], in_=ident[:, 0:1])
+            if step + 1 < SLOTS:
+                regroup(step + 1)
+            if step == STEPS - 1:
+                sum_e = const.tile([P, HALVES, B], F32)
+                nc.vector.tensor_reduce(out=sum_e[:], in_=sum_e4[:], axis=AX.X, op=ALU.add)
+                nc.vector.reciprocal(out=inv_e[:], in_=sum_e[:])
+                nc.vector.tensor_mul(out=v[:, 0:HALVES, 0:B], in0=sum_ex[:], in1=inv_e[:])
+                nc.vector.tensor_mul(
+                    out=mean_sq[:], in0=v[:, 0:HALVES, 0:B], in1=v[:, 0:HALVES, 0:B]
+                )
+            product(step)
+            if 1 <= step <= SLOTS:
+                chunk_max(step - 1)
 
         spread = const.tile([P, HALVES, B], F32)
         nc.vector.tensor_mul(out=spread[:], in0=sum_exx[:], in1=inv_e[:])
@@ -270,14 +308,14 @@ def tile_attentivestatspool_pb_t_kernel(
         nc.vector.tensor_scalar_max(out=spread[:], in0=spread[:], scalar1=EPS_STD)
         nc.scalar.sqrt(out=v[:, HALVES : 2 * HALVES, 0:B], in_=spread[:])
 
-        turned = tail_psum.tile([P, 2 * C], F32)
+        pooled = back_pool.tile([P, 2 * C], F32, name="back")
         for q in range(2 * HALVES):
             nc.tensor.transpose(
-                out=turned[:, q * P : (q + 1) * P], in_=v[:, q, :], identity=ident[:]
+                out=pooled[:, q * P : (q + 1) * P], in_=v[:, q, :], identity=ident[:]
             )
 
         stats = const.tile([B, 6], F32)
-        nc.vector.bn_stats(out=stats[:], in_=turned[0:B, :])
+        nc.vector.bn_stats(out=stats[:], in_=pooled[0:B, :])
         mean_var = const.tile([B, 2], F32)
         nc.vector.bn_aggr(out=mean_var[:], in_=stats[:])
         sd = const.tile([B, 1], F32)
@@ -288,7 +326,7 @@ def tile_attentivestatspool_pb_t_kernel(
         result = const.tile([B, 2 * C], F32)
         nc.vector.scalar_tensor_tensor(
             out=result[:],
-            in0=turned[0:B, :],
+            in0=pooled[0:B, :],
             scalar=mean_var[:, 0:1],
             in1=gain[:],
             op0=ALU.subtract,

@@ -36,8 +36,9 @@ EXP_LAG = 5
 PRODUCT_LAG = 7
 STEPS = SLOTS + PRODUCT_LAG
 EARLY_SLOTS = 8
-EARLY_FRAMES = 512
-LATE_FRAMES = 336
+EARLY_FRAMES = 384
+LATE_FRAMES = 256
+GPSIMD_FRAMES = 128
 
 
 def tile_attentivestatspool_pb_t_kernel(
@@ -46,7 +47,7 @@ def tile_attentivestatspool_pb_t_kernel(
     nc = tc.nc
     with tc.tile_pool(name="const", bufs=1) as const, tc.tile_pool(
         name="raw", bufs=8
-    ) as raw_pool, tc.tile_pool(name="grouped", bufs=3) as grouped_pool, tc.tile_pool(
+    ) as raw_pool, tc.tile_pool(name="grouped", bufs=2) as grouped_pool, tc.tile_pool(
         name="quant", bufs=3
     ) as quant, tc.tile_pool(name="turned", bufs=2) as turned_pool, tc.tile_pool(
         name="feat", bufs=3
@@ -92,20 +93,37 @@ def tile_attentivestatspool_pb_t_kernel(
             x_sb[b] = feat.tile([P, HALVES, T], BF16, name="x_sb")
             nc.sync.dma_start(out=x_sb[b][:], in_=x[b].rearrange("(hf p) n -> p hf n", p=P))
 
-        def regroup(s):
+        def views(s, g):
+            dst = grouped[s][:, g].rearrange("p (c i) j -> p c j i", i=4)
+            src = raw[s, g][:].rearrange("p j (c i) -> p c j i", i=4)
+            return dst, src
+
+        def regroup_start(s):
             grouped[s] = grouped_pool.tile(
                 [P, PASSES, FRAMES, PACK], BF16, name="grouped", align_bytes=64
             )
+            if s >= 2:
+                f = FRAMES - GPSIMD_FRAMES
+                nc.gpsimd.tensor_scalar(
+                    out=grouped[s][:, 1, f:, :],
+                    in0=raw[s, 1][:, :, f:].rearrange("p j n -> p n j"),
+                    scalar1=1.0,
+                    scalar2=0.0,
+                    op0=ALU.mult,
+                    op1=ALU.add,
+                )
+
+        def regroup_first_pass(s):
+            dst, src = views(s, 0)
+            nc.scalar.copy(out=dst, in_=src)
+
+        def regroup_second_pass(s):
+            dst, src = views(s, 1)
+            end = (FRAMES - (GPSIMD_FRAMES if s >= 2 else 0)) // 4
             cut = (EARLY_FRAMES if s < EARLY_SLOTS else LATE_FRAMES) // 4
-            for g in range(PASSES):
-                dst = grouped[s][:, g].rearrange("p (c i) j -> p c j i", i=4)
-                src = raw[s, g][:].rearrange("p j (c i) -> p c j i", i=4)
-                if g == 0:
-                    nc.scalar.copy(out=dst, in_=src)
-                else:
-                    nc.vector.tensor_copy(out=dst[:, 0:cut], in_=src[:, 0:cut])
-                    if cut < FRAMES // 4:
-                        nc.scalar.copy(out=dst[:, cut:], in_=src[:, cut:])
+            nc.vector.tensor_copy(out=dst[:, 0:cut], in_=src[:, 0:cut])
+            if cut < end:
+                nc.scalar.copy(out=dst[:, cut:end], in_=src[:, cut:end])
 
         def quantise(s):
             codes[s] = quant.tile([P, PASSES * FRAMES], U32, name="codes", align_bytes=64)
@@ -249,7 +267,10 @@ def tile_attentivestatspool_pb_t_kernel(
         mask_cols = back_pool.tile([P, P], BF16, name="back")
         nc.tensor.transpose(out=mask_cols[:], in_=mask_rows[:], identity=ident_bf[:])
         penalty = const.tile([P, B * UTT_TILES], F32)
-        regroup(0)
+        regroup_start(0)
+        regroup_first_pass(0)
+        regroup_second_pass(0)
+        regroup_start(1)
 
         warm = const.tile([P, 1], F32)
         inv_e = const.tile([P, HALVES, B], F32)
@@ -264,8 +285,6 @@ def tile_attentivestatspool_pb_t_kernel(
             if step == SLOTS - 1:
                 nc.sync.dma_start(out=gain[:], in_=g2.partition_broadcast(B))
                 nc.sync.dma_start(out=offset[:], in_=be2.partition_broadcast(B))
-            if 1 <= step <= SLOTS:
-                empty(step - 1)
             now = units(step)
             for b, c, hf in now:
                 again[b, c, hf] = turn(b, c, hf)
@@ -281,15 +300,22 @@ def tile_attentivestatspool_pb_t_kernel(
                     op0=ALU.mult,
                     op1=ALU.add,
                 )
+            if step + 2 < SLOTS:
+                regroup_start(step + 2)
             if 1 <= step <= SLOTS:
-                for hf in range(HALVES):
-                    first[step - 1, hf] = turn((step - 1) // CHUNKS, (step - 1) % CHUNKS, hf)
+                chunk_max(step - 1)
+            if step + 1 < SLOTS:
+                regroup_first_pass(step + 1)
             for b, c, hf in now:
                 exponent(b, c, hf)
+            if step < SLOTS:
+                empty(step)
+                for hf in range(HALVES):
+                    first[step, hf] = turn(step // CHUNKS, step % CHUNKS, hf)
             if step == CHUNKS * (B - 1) + EXP_LAG + CHUNKS - 1:
                 nc.scalar.sqrt(out=warm[:], in_=ident[:, 0:1])
             if step + 1 < SLOTS:
-                regroup(step + 1)
+                regroup_second_pass(step + 1)
             if step == STEPS - 1:
                 sum_e = const.tile([P, HALVES, B], F32)
                 nc.vector.tensor_reduce(out=sum_e[:], in_=sum_e4[:], axis=AX.X, op=ALU.add)
@@ -299,8 +325,6 @@ def tile_attentivestatspool_pb_t_kernel(
                     out=mean_sq[:], in0=v[:, 0:HALVES, 0:B], in1=v[:, 0:HALVES, 0:B]
                 )
             product(step)
-            if 1 <= step <= SLOTS:
-                chunk_max(step - 1)
 
         spread = const.tile([P, HALVES, B], F32)
         nc.vector.tensor_mul(out=spread[:], in0=sum_exx[:], in1=inv_e[:])

@@ -39,6 +39,8 @@ EARLY_SLOTS = 8
 EARLY_FRAMES = 384
 LATE_FRAMES = 256
 GPSIMD_FRAMES = 128
+BRIDGE_FRAMES = 208
+HEAD_FRAMES = 320
 
 
 def tile_attentivestatspool_pb_t_kernel(
@@ -113,15 +115,24 @@ def tile_attentivestatspool_pb_t_kernel(
                     op1=ALU.add,
                 )
 
+        def bridge(s):
+            return EXP_LAG < s < EARLY_SLOTS
+
         def regroup_first_pass(s):
             dst, src = views(s, 0)
-            nc.scalar.copy(out=dst, in_=src)
+            cut = (BRIDGE_FRAMES if bridge(s) else 0) // 4
+            nc.scalar.copy(out=dst[:, cut:], in_=src[:, cut:])
 
         def regroup_second_pass(s):
             dst, src = views(s, 1)
             end = (FRAMES - (GPSIMD_FRAMES if s >= 2 else 0)) // 4
             cut = (EARLY_FRAMES if s < EARLY_SLOTS else LATE_FRAMES) // 4
             nc.vector.tensor_copy(out=dst[:, 0:cut], in_=src[:, 0:cut])
+            if bridge(s):
+                dst0, src0 = views(s, 0)
+                nc.vector.tensor_copy(
+                    out=dst0[:, 0 : BRIDGE_FRAMES // 4], in_=src0[:, 0 : BRIDGE_FRAMES // 4]
+                )
             if cut < end:
                 nc.scalar.copy(out=dst[:, cut:end], in_=src[:, cut:end])
 
@@ -268,8 +279,12 @@ def tile_attentivestatspool_pb_t_kernel(
         nc.tensor.transpose(out=mask_cols[:], in_=mask_rows[:], identity=ident_bf[:])
         penalty = const.tile([P, B * UTT_TILES], F32)
         regroup_start(0)
-        regroup_first_pass(0)
-        regroup_second_pass(0)
+        for g in range(PASSES):
+            dst, src = views(0, g)
+            nc.vector.tensor_copy(
+                out=dst[:, 0 : HEAD_FRAMES // 4], in_=src[:, 0 : HEAD_FRAMES // 4]
+            )
+            nc.scalar.copy(out=dst[:, HEAD_FRAMES // 4 :], in_=src[:, HEAD_FRAMES // 4 :])
         regroup_start(1)
 
         warm = const.tile([P, 1], F32)
@@ -277,6 +292,7 @@ def tile_attentivestatspool_pb_t_kernel(
         mean_sq = const.tile([P, HALVES, B], F32)
         gain = const.tile([B, 2 * C], BF16)
         offset = const.tile([B, 2 * C], BF16)
+        stats = const.tile([B, 2, 6], F32)
         for step in range(STEPS):
             if step + LOAD_AHEAD < SLOTS:
                 load(step + LOAD_AHEAD)
@@ -317,6 +333,7 @@ def tile_attentivestatspool_pb_t_kernel(
             if step + 1 < SLOTS:
                 regroup_second_pass(step + 1)
             if step == STEPS - 1:
+                pooled = back_pool.tile([P, 2 * C], F32, name="back")
                 sum_e = const.tile([P, HALVES, B], F32)
                 nc.vector.tensor_reduce(out=sum_e[:], in_=sum_e4[:], axis=AX.X, op=ALU.add)
                 nc.vector.reciprocal(out=inv_e[:], in_=sum_e[:])
@@ -324,6 +341,10 @@ def tile_attentivestatspool_pb_t_kernel(
                 nc.vector.tensor_mul(
                     out=mean_sq[:], in0=v[:, 0:HALVES, 0:B], in1=v[:, 0:HALVES, 0:B]
                 )
+                for q in range(HALVES):
+                    nc.tensor.transpose(
+                        out=pooled[:, q * P : (q + 1) * P], in_=v[:, q, :], identity=ident[:]
+                    )
             product(step)
 
         spread = const.tile([P, HALVES, B], F32)
@@ -332,21 +353,18 @@ def tile_attentivestatspool_pb_t_kernel(
         nc.vector.tensor_scalar_max(out=spread[:], in0=spread[:], scalar1=EPS_STD)
         nc.scalar.sqrt(out=v[:, HALVES : 2 * HALVES, 0:B], in_=spread[:])
 
-        pooled = back_pool.tile([P, 2 * C], F32, name="back")
-        for q in range(2 * HALVES):
+        nc.vector.bn_stats(out=stats[:, 0, :], in_=pooled[0:B, 0:C])
+        for q in range(HALVES, 2 * HALVES):
             nc.tensor.transpose(
                 out=pooled[:, q * P : (q + 1) * P], in_=v[:, q, :], identity=ident[:]
             )
 
-        stats = const.tile([B, 6], F32)
-        nc.vector.bn_stats(out=stats[:], in_=pooled[0:B, :])
+        nc.vector.bn_stats(out=stats[:, 1, :], in_=pooled[0:B, C : 2 * C])
         mean_var = const.tile([B, 2], F32)
         nc.vector.bn_aggr(out=mean_var[:], in_=stats[:])
         sd = const.tile([B, 1], F32)
         nc.vector.tensor_scalar_add(out=sd[:], in0=mean_var[:, 1:2], scalar1=EPS_LN)
         nc.scalar.sqrt(out=sd[:], in_=sd[:])
-        inv_sd = const.tile([B, 1], F32)
-        nc.vector.reciprocal(out=inv_sd[:], in_=sd[:])
         result = const.tile([B, 2 * C], F32)
         nc.vector.scalar_tensor_tensor(
             out=result[:],
@@ -356,6 +374,8 @@ def tile_attentivestatspool_pb_t_kernel(
             op0=ALU.subtract,
             op1=ALU.mult,
         )
+        inv_sd = const.tile([B, 1], F32)
+        nc.vector.reciprocal(out=inv_sd[:], in_=sd[:])
         nc.vector.scalar_tensor_tensor(
             out=result[:],
             in0=result[:],

@@ -32,10 +32,10 @@ MASKED = 1.0e30
 
 SLOTS = B * CHUNKS
 LOAD_AHEAD = 3
-EXP_LAG = 5
-PRODUCT_LAG = 7
+EXP_LAG = 4
+PRODUCT_LAG = 6
 STEPS = SLOTS + PRODUCT_LAG
-EARLY_SLOTS = 8
+EARLY_SLOTS = 7
 EARLY_FRAMES = 384
 LATE_FRAMES = 256
 GPSIMD_FRAMES = 128
@@ -302,11 +302,11 @@ def tile_attentivestatspool_pb_t_kernel(
                 nc.sync.dma_start(out=gain[:], in_=g2.partition_broadcast(B))
                 nc.sync.dma_start(out=offset[:], in_=be2.partition_broadcast(B))
             now = units(step)
-            for b, c, hf in now:
-                again[b, c, hf] = turn(b, c, hf)
             if step < SLOTS:
                 quantise(step)
                 multiply(step)
+            for b, c, hf in now:
+                again[b, c, hf] = turn(b, c, hf)
             if step == 0:
                 nc.vector.tensor_scalar(
                     out=penalty[:],
@@ -322,16 +322,15 @@ def tile_attentivestatspool_pb_t_kernel(
                 chunk_max(step - 1)
             if step + 1 < SLOTS:
                 regroup_first_pass(step + 1)
-            for b, c, hf in now:
-                exponent(b, c, hf)
+                regroup_second_pass(step + 1)
             if step < SLOTS:
                 empty(step)
                 for hf in range(HALVES):
                     first[step, hf] = turn(step // CHUNKS, step % CHUNKS, hf)
+            for b, c, hf in now:
+                exponent(b, c, hf)
             if step == CHUNKS * (B - 1) + EXP_LAG + CHUNKS - 1:
                 nc.scalar.sqrt(out=warm[:], in_=ident[:, 0:1])
-            if step + 1 < SLOTS:
-                regroup_second_pass(step + 1)
             if step == STEPS - 1:
                 pooled = back_pool.tile([P, 2 * C], F32, name="back")
                 sum_e = const.tile([P, HALVES, B], F32)

import concourse.bass as bass
import concourse.mybir as mybir
import concourse.tile as tile
from concourse.masks import make_identity

FLOPS = 2 * 4 * 256 * 1024 * 2048

F32 = mybir.dt.float32
BF16 = mybir.dt.bfloat16
I32 = mybir.dt.int32
U32 = mybir.dt.uint32
U8 = mybir.dt.uint8
FP8X4 = mybir.dt.float8_e4m3fn_x4
FP4X4 = mybir.dt.float4_e2m1fn_x4
ALU = mybir.AluOpType
ACT = mybir.ActivationFunctionType
AX = mybir.AxisListType

P = 128
PACK = 4
K_PASS = P * PACK
B, C, T, H = 4, 256, 2048, 1024
PASSES = H // K_PASS
HALVES = C // P
FRAMES = 512
CHUNKS = T // FRAMES
TILES = FRAMES // P
UTT_TILES = T // P
EPS_LN = 1e-5
EPS_STD = 1e-5
MASKED = 1.0e30

SLOTS = B * CHUNKS
LOAD_AHEAD = 3
EXP_LAG = 4
PRODUCT_LAG = 6
STEPS = SLOTS + PRODUCT_LAG
EARLY_SLOTS = 7
EARLY_FRAMES = 384
LATE_FRAMES = 256
GPSIMD_FRAMES = 128
BRIDGE_FRAMES = 208
HEAD_FRAMES = 320


def tile_attentivestatspool_pb_t_kernel(
    tc, h, x, mask, w2_words, w2_scales, b2, g2, be2, out
):
    nc = tc.nc
    with tc.tile_pool(name="const", bufs=1) as const, tc.tile_pool(
        name="raw", bufs=8
    ) as raw_pool, tc.tile_pool(name="grouped", bufs=2) as grouped_pool, tc.tile_pool(
        name="quant", bufs=3
    ) as quant, tc.tile_pool(name="turned", bufs=2) as turned_pool, tc.tile_pool(
        name="feat", bufs=3
    ) as feat, tc.tile_pool(name="score", bufs=4) as score, tc.tile_pool(
        name="prod", bufs=2
    ) as prod, tc.psum_pool(name="acc", bufs=4) as acc_pool, tc.psum_pool(
        name="back", bufs=4
    ) as back_pool, tc.manual_schedule():
        ident = const.tile([P, P], F32)
        make_identity(nc, ident[:])
        ident_bf = const.tile([P, P], BF16)
        make_identity(nc, ident_bf[:])
        v = const.tile([P, 2 * HALVES, P], F32)
        nc.gpsimd.memset(v[:], 0.0)
        sum_e4 = const.tile([P, HALVES, B, CHUNKS], F32)
        sum_ex = const.tile([P, HALVES, B], F32)
        sum_exx = const.tile([P, HALVES, B], F32)
        neg_max4 = const.tile([P, B, HALVES, CHUNKS], F32)
        neg_max = const.tile([P, B, HALVES], F32)

        raw = {}
        grouped = {}
        codes = {}
        planes = {}
        acc = {}
        turned = {}
        first = {}
        again = {}
        x_sb = {}
        e = {}
        ex = {}

        def load(s):
            b, c = divmod(s, CHUNKS)
            h_rows = h[b].rearrange("(g p j) n -> g p j n", p=P, j=PACK)
            for g in range(PASSES):
                raw[s, g] = raw_pool.tile([P, PACK, FRAMES], BF16, name="raw")
                nc.sync.dma_start(
                    out=raw[s, g][:], in_=h_rows[g, :, :, c * FRAMES : (c + 1) * FRAMES]
                )

        def load_x(b):
            x_sb[b] = feat.tile([P, HALVES, T], BF16, name="x_sb")
            nc.sync.dma_start(out=x_sb[b][:], in_=x[b].rearrange("(hf p) n -> p hf n", p=P))

        def views(s, g):
            dst = grouped[s][:, g].rearrange("p (c i) j -> p c j i", i=4)
            src = raw[s, g][:].rearrange("p j (c i) -> p c j i", i=4)
            return dst, src

        def regroup_start(s):
            grouped[s] = grouped_pool.tile(
                [P, PASSES, FRAMES, PACK], BF16, name="grouped", align_bytes=64
            )
            if s >= 2:
                f = FRAMES - GPSIMD_FRAMES
                nc.gpsimd.tensor_scalar(
                    out=grouped[s][:, 1, f:, :],
                    in0=raw[s, 1][:, :, f:].rearrange("p j n -> p n j"),
                    scalar1=1.0,
                    scalar2=0.0,
                    op0=ALU.mult,
                    op1=ALU.add,
                )

        def bridge(s):
            return EXP_LAG < s < EARLY_SLOTS

        def regroup_first_pass(s):
            dst, src = views(s, 0)
            cut = (BRIDGE_FRAMES if bridge(s) else 0) // 4
            nc.scalar.copy(out=dst[:, cut:], in_=src[:, cut:])

        def regroup_second_pass(s):
            dst, src = views(s, 1)
            end = (FRAMES - (GPSIMD_FRAMES if s >= 2 else 0)) // 4
            cut = (EARLY_FRAMES if s < EARLY_SLOTS else LATE_FRAMES) // 4
            nc.vector.tensor_copy(out=dst[:, 0:cut], in_=src[:, 0:cut])
            if bridge(s):
                dst0, src0 = views(s, 0)
                nc.vector.tensor_copy(
                    out=dst0[:, 0 : BRIDGE_FRAMES // 4], in_=src0[:, 0 : BRIDGE_FRAMES // 4]
                )
            if cut < end:
                nc.scalar.copy(out=dst[:, cut:end], in_=src[:, cut:end])

        def quantise(s):
            codes[s] = quant.tile([P, PASSES * FRAMES], U32, name="codes", align_bytes=64)
            planes[s] = quant.tile([P, PASSES * FRAMES], U8, name="planes", align_bytes=64)
            nc.vector.quantize_mx(
                out=codes[s][:].bitcast(FP8X4),
                scales=planes[s][:],
                in_=grouped[s][:].rearrange("p g n j -> p (g n j)"),
            )

        def multiply(s):
            for k in range(TILES // 2):
                acc[s, k] = acc_pool.tile([P, 2 * C], F32, name="acc")
            for i in range(TILES):
                for hf in range(HALVES):
                    for g in range(PASSES):
                        cols = slice(g * FRAMES + i * P, g * FRAMES + (i + 1) * P)
                        at = (i % 2) * C + hf * P
                        nc.tensor.matmul_mx(
                            out=acc[s, i // 2][:, at : at + P],
                            lhsT=codes[s][:, cols].bitcast(FP8X4),
                            lhsT_scale=planes[s][:, cols],
                            rhs=w_words[:, g, 2 * P * hf : 2 * P * (hf + 1)].bitcast(FP4X4),
                            rhs_scale=w_planes[:, g, P * hf : P * (hf + 1)],
                            start=(g == 0),
                            stop=(g == PASSES - 1),
                        )

        def empty(s):
            b, c = divmod(s, CHUNKS)
            if c == 0:
                turned[b] = turned_pool.tile([P, UTT_TILES, C], F32, name="turned")
            for i in range(TILES):
                n = c * TILES + i
                nc.scalar.activation(
                    out=turned[b][:, n, :],
                    in_=acc[s, i // 2][:, (i % 2) * C : (i % 2 + 1) * C],
                    func=ACT.Identity,
                    bias=penalty[:, b * UTT_TILES + n : b * UTT_TILES + n + 1],
                    scale=1.0,
                )

        def turn(b, c, hf):
            bank = back_pool.tile([P, FRAMES], F32, name="back")
            for i in range(TILES):
                nc.tensor.transpose(
                    out=bank[:, i * P : (i + 1) * P],
                    in_=turned[b][:, c * TILES + i, hf * P : (hf + 1) * P],
                    identity=ident[:],
                )
            return bank

        def chunk_max(s):
            b, c = divmod(s, CHUNKS)
            for hf in range(HALVES):
                nc.vector.tensor_reduce(
                    out=neg_max4[:, b, hf, c : c + 1],
                    in_=first[s, hf][:],
                    axis=AX.X,
                    op=ALU.max,
                    negate=True,
                )
            if c == CHUNKS - 1:
                nc.vector.tensor_reduce(
                    out=neg_max[:, b, :], in_=neg_max4[:, b], axis=AX.X, op=ALU.min
                )

        def units(step):
            found = []
            for b in range(B):
                k = 2 * (step - CHUNKS * b - EXP_LAG)
                if 0 <= k < HALVES * CHUNKS:
                    found.extend([(b, n % CHUNKS, n // CHUNKS) for n in (k, k + 1)])
            return found

        def exponent(b, c, hf):
            if c == 0:
                e[b, hf] = score.tile([P, T], F32, name="e")
            nc.scalar.activation(
                out=e[b, hf][:, c * FRAMES : (c + 1) * FRAMES],
                in_=again[b, c, hf][:],
                func=ACT.Exp,
                bias=neg_max[:, b, hf : hf + 1],
                scale=1.0,
                accum_out=sum_e4[:, hf, b, c : c + 1],
            )

        def product(step):
            n = step - PRODUCT_LAG
            if n < 0 or n >= 2 * HALVES * B:
                return
            b, k = divmod(n, 2 * HALVES)
            hf, second = divmod(k, 2)
            if not second:
                ex[b, hf] = prod.tile([P, T], F32, name="ex")
                nc.vector.scalar_tensor_tensor(
                    out=ex[b, hf][:],
                    in0=e[b, hf][:],
                    scalar=1.0,
                    in1=x_sb[b][:, hf, :],
                    op0=ALU.mult,
                    op1=ALU.mult,
                    accum_out=sum_ex[:, hf, b : b + 1],
                )
            else:
                exx = prod.tile([P, T], F32, name="exx")
                nc.vector.scalar_tensor_tensor(
                    out=exx[:],
                    in0=ex[b, hf][:],
                    scalar=1.0,
                    in1=x_sb[b][:, hf, :],
                    op0=ALU.mult,
                    op1=ALU.mult,
                    accum_out=sum_exx[:, hf, b : b + 1],
                )

        load(0)
        load(1)
        mask_rows = const.tile([P, P], BF16)
        nc.vector.memset(mask_rows[B * UTT_TILES : P, :], 0.0)
        nc.sync.dma_start(
            out=mask_rows[0 : B * UTT_TILES, :],
            in_=mask.rearrange("b o (i p) -> (b o i) p", p=P),
        )
        w_words = const.tile([P, PASSES, 2 * C], U8, align_bytes=64)
        nc.sync.dma_start(
            out=w_words[:].bitcast(I32),
            in_=w2_words.bitcast(I32).rearrange("g p n -> p g n"),
        )
        w_planes = const.tile([P, PASSES, C], U8, align_bytes=64)
        nc.vector.memset(w_planes[:].rearrange("p g n -> p (g n)").bitcast(I32), 0)
        for q in range(4):
            nc.sync.dma_start(
                out=w_planes[32 * q : 32 * q + 4].bitcast(I32),
                in_=w2_scales.bitcast(I32)[:, 4 * q : 4 * q + 4, :].rearrange(
                    "g r n -> r g n"
                ),
            )
        for s in range(2, LOAD_AHEAD):
            load(s)
        mask_cols = back_pool.tile([P, P], BF16, name="back")
        nc.tensor.transpose(out=mask_cols[:], in_=mask_rows[:], identity=ident_bf[:])
        penalty = const.tile([P, B * UTT_TILES], F32)
        regroup_start(0)
        for g in range(PASSES):
            dst, src = views(0, g)
            nc.vector.tensor_copy(
                out=dst[:, 0 : HEAD_FRAMES // 4], in_=src[:, 0 : HEAD_FRAMES // 4]
            )
            nc.scalar.copy(out=dst[:, HEAD_FRAMES // 4 :], in_=src[:, HEAD_FRAMES // 4 :])
        regroup_start(1)

        warm = const.tile([P, 1], F32)
        inv_e = const.tile([P, HALVES, B], F32)
        mean_sq = const.tile([P, HALVES, B], F32)
        gain = const.tile([B, 2 * C], BF16)
        offset = const.tile([B, 2 * C], BF16)
        stats = const.tile([B, 2, 6], F32)
        for step in range(STEPS):
            if step + LOAD_AHEAD < SLOTS:
                load(step + LOAD_AHEAD)
            if step < SLOTS and step % CHUNKS == CHUNKS - 1:
                load_x(step // CHUNKS)
            if step == SLOTS - 1:
                nc.sync.dma_start(out=gain[:], in_=g2.partition_broadcast(B))
                nc.sync.dma_start(out=offset[:], in_=be2.partition_broadcast(B))
            now = units(step)
            if step < SLOTS:
                quantise(step)
                multiply(step)
            for b, c, hf in now:
                again[b, c, hf] = turn(b, c, hf)
            if step == 0:
                nc.vector.tensor_scalar(
                    out=penalty[:],
                    in0=mask_cols[:, 0 : B * UTT_TILES],
                    scalar1=MASKED,
                    scalar2=-MASKED,
                    op0=ALU.mult,
                    op1=ALU.add,
                )
            if step + 2 < SLOTS:
                regroup_start(step + 2)
            if 1 <= step <= SLOTS:
                chunk_max(step - 1)
            if step + 1 < SLOTS:
                regroup_first_pass(step + 1)
                regroup_second_pass(step + 1)
            if step < SLOTS:
                empty(step)
                for hf in range(HALVES):
                    first[step, hf] = turn(step // CHUNKS, step % CHUNKS, hf)
            for b, c, hf in now:
                exponent(b, c, hf)
            if step == CHUNKS * (B - 1) + EXP_LAG + CHUNKS - 1:
                nc.scalar.sqrt(out=warm[:], in_=ident[:, 0:1])
            if step == STEPS - 1:
                pooled = back_pool.tile([P, 2 * C], F32, name="back")
                sum_e = const.tile([P, HALVES, B], F32)
                nc.vector.tensor_reduce(out=sum_e[:], in_=sum_e4[:], axis=AX.X, op=ALU.add)
                nc.vector.reciprocal(out=inv_e[:], in_=sum_e[:])
                nc.vector.tensor_mul(out=v[:, 0:HALVES, 0:B], in0=sum_ex[:], in1=inv_e[:])
                nc.vector.tensor_mul(
                    out=mean_sq[:], in0=v[:, 0:HALVES, 0:B], in1=v[:, 0:HALVES, 0:B]
                )
                for q in range(HALVES):
                    nc.tensor.transpose(
                        out=pooled[:, q * P : (q + 1) * P], in_=v[:, q, :], identity=ident[:]
                    )
            product(step)

        spread = const.tile([P, HALVES, B], F32)
        nc.vector.tensor_mul(out=spread[:], in0=sum_exx[:], in1=inv_e[:])
        nc.vector.tensor_sub(out=spread[:], in0=spread[:], in1=mean_sq[:])
        nc.vector.tensor_scalar_max(out=spread[:], in0=spread[:], scalar1=EPS_STD)
        nc.scalar.sqrt(out=v[:, HALVES : 2 * HALVES, 0:B], in_=spread[:])

        nc.vector.bn_stats(out=stats[:, 0, :], in_=pooled[0:B, 0:C])
        for q in range(HALVES, 2 * HALVES):
            nc.tensor.transpose(
                out=pooled[:, q * P : (q + 1) * P], in_=v[:, q, :], identity=ident[:]
            )

        nc.vector.bn_stats(out=stats[:, 1, :], in_=pooled[0:B, C : 2 * C])
        mean_var = const.tile([B, 2], F32)
        nc.vector.bn_aggr(out=mean_var[:], in_=stats[:])
        sd = const.tile([B, 1], F32)
        nc.vector.tensor_scalar_add(out=sd[:], in0=mean_var[:, 1:2], scalar1=EPS_LN)
        nc.scalar.sqrt(out=sd[:], in_=sd[:])
        result = const.tile([B, 2 * C], F32)
        nc.vector.scalar_tensor_tensor(
            out=result[:],
            in0=pooled[0:B, :],
            scalar=mean_var[:, 0:1],
            in1=gain[:],
            op0=ALU.subtract,
            op1=ALU.mult,
        )
        inv_sd = const.tile([B, 1], F32)
        nc.vector.reciprocal(out=inv_sd[:], in_=sd[:])
        nc.vector.scalar_tensor_tensor(
            out=result[:],
            in0=result[:],
            scalar=inv_sd[:],
            in1=offset[:],
            op0=ALU.mult,
            op1=ALU.add,
        )
        nc.sync.dma_start(out=out.rearrange("b n o -> b (n o)"), in_=result[:])
